import numpy as np
import ml_dtypes

BF16 = ml_dtypes.bfloat16


def bf(x):
    return np.asarray(x, np.float32).astype(BF16)


def f32(x):
    return np.asarray(x, np.float32)


def f64(x):
    return np.asarray(x).astype(np.float64)


def striped(idx):
    return np.tile(idx.reshape(-1, 16).T, (8, 1))


C, S, N, M = 1024, 512, 256, 128


def setup_inputs():
    return {"base": f32(np.abs(np.random.standard_normal((C, S)))), "hl": f32(np.random.standard_normal((C, M))), "hr": f32(np.random.standard_normal((C, M))), "offs": striped(np.random.permutation(S)[:N])}


def reference(base, hl, hr, offs):
    idx = offs[:16].T.reshape(-1)
    d = f64(hl) + (-f64(hr))
    v = d * np.sign(d)
    out = f64(base).copy()
    out[:, idx[:M]] = v
    out[:, idx[M:]] = v
    return out

@@ -1,0 +1,49 @@
+import concourse.mybir as mybir
+
+F32 = mybir.dt.float32
+U16 = mybir.dt.uint16
+MULT = mybir.AluOpType.mult
+P = 128
+PER_COLUMN = 16
+
+
+def tile_symbranch_s_kernel(tc, base, hl, hr, offs, out):
+    nc = tc.nc
+    features, nodes = base.shape
+    pairs = hl.shape[1]
+    n_blocks = features // P
+    pair_columns = pairs // PER_COLUMN
+
+    base_blocks = base.rearrange("(b p) s -> b p s", p=P)
+    hl_blocks = hl.rearrange("(b p) m -> b p m", p=P)
+    hr_blocks = hr.rearrange("(b p) m -> b p m", p=P)
+    out_blocks = out.rearrange("(b p) s -> b p s", p=P)
+
+    with (
+        tc.tile_pool(name="held", bufs=1) as held,
+        tc.tile_pool(name="blocks", bufs=n_blocks) as blocks,
+    ):
+        offsets = held.tile([P, offs.shape[1]], U16, name="offsets")
+        nc.sync.dma_start(offsets[:], offs)
+
+        lefts, rights, windows = [], [], []
+        for b in range(n_blocks):
+            left = blocks.tile([P, pairs], F32, name="left")
+            right = blocks.tile([P, pairs], F32, name="right")
+            window = blocks.tile([P, nodes], F32, name="window")
+            nc.scalar.dma_start(left[:], hl_blocks[b])
+            nc.scalar.dma_start(right[:], hr_blocks[b])
+            nc.sync.dma_start(window[:], base_blocks[b])
+            lefts.append(left)
+            rights.append(right)
+            windows.append(window)
+
+        for b in range(n_blocks):
+            diff = blocks.tile([P, pairs], F32, name="diff")
+            sign = blocks.tile([P, pairs], F32, name="sign")
+            nc.vector.tensor_sub(diff[:], lefts[b][:], rights[b][:])
+            nc.scalar.sign(sign[:], diff[:])
+            for side in range(2):
+                places = offsets[:, side * pair_columns : (side + 1) * pair_columns]
+                nc.vector.tensor_tensor(windows[b][:].indirect(places), diff[:], sign[:], MULT)
+            nc.sync.dma_start(out_blocks[b], windows[b][:])

@@ -14,36 +14,45 @@ def tile_symbranch_s_kernel(tc, base, hl, hr, offs, out):
     n_blocks = features // P
     pair_columns = pairs // PER_COLUMN
 
-    base_blocks = base.rearrange("(b p) s -> b p s", p=P)
-    hl_blocks = hl.rearrange("(b p) m -> b p m", p=P)
-    hr_blocks = hr.rearrange("(b p) m -> b p m", p=P)
-    out_blocks = out.rearrange("(b p) s -> b p s", p=P)
+    base_blocks = base.rearrange("(p b) s -> b p s", b=n_blocks)
+    out_blocks = out.rearrange("(p b) s -> b p s", b=n_blocks)
+    hl_rows = hl.rearrange("(p b) m -> p (b m)", b=n_blocks)
+    hr_rows = hr.rearrange("(p b) m -> p (b m)", b=n_blocks)
+
+    pieces = []
+    first = 0
+    while first < n_blocks:
+        behind = first + max(first, 1)
+        pieces.append((first, behind))
+        first = behind
 
     with (
         tc.tile_pool(name="held", bufs=1) as held,
         tc.tile_pool(name="blocks", bufs=n_blocks) as blocks,
     ):
         offsets = held.tile([P, offs.shape[1]], U16, name="offsets")
+        left = held.tile([P, n_blocks * pairs], F32, name="left")
+        right = held.tile([P, n_blocks * pairs], F32, name="right")
+        diff = held.tile([P, n_blocks * pairs], F32, name="diff")
+        sign = held.tile([P, n_blocks * pairs], F32, name="sign")
+        windows = [blocks.tile([P, nodes], F32, name="window") for b in range(n_blocks)]
+
         nc.sync.dma_start(offsets[:], offs)
+        for first, behind in pieces:
+            columns = slice(first * pairs, behind * pairs)
+            nc.sync.dma_start(left[:, columns], hl_rows[:, columns])
+            nc.sync.dma_start(right[:, columns], hr_rows[:, columns])
+            for b in range(first, behind):
+                nc.sync.dma_start(windows[b][:], base_blocks[b])
 
-        lefts, rights, windows = [], [], []
-        for b in range(n_blocks):
-            left = blocks.tile([P, pairs], F32, name="left")
-            right = blocks.tile([P, pairs], F32, name="right")
-            window = blocks.tile([P, nodes], F32, name="window")
-            nc.scalar.dma_start(left[:], hl_blocks[b])
-            nc.scalar.dma_start(right[:], hr_blocks[b])
-            nc.sync.dma_start(window[:], base_blocks[b])
-            lefts.append(left)
-            rights.append(right)
-            windows.append(window)
+        for first, behind in pieces:
+            columns = slice(first * pairs, behind * pairs)
+            nc.vector.tensor_sub(diff[:, columns], left[:, columns], right[:, columns])
+            nc.scalar.sign(sign[:, columns], diff[:, columns])
 
         for b in range(n_blocks):
-            diff = blocks.tile([P, pairs], F32, name="diff")
-            sign = blocks.tile([P, pairs], F32, name="sign")
-            nc.vector.tensor_sub(diff[:], lefts[b][:], rights[b][:])
-            nc.scalar.sign(sign[:], diff[:])
+            block = slice(b * pairs, (b + 1) * pairs)
             for side in range(2):
                 places = offsets[:, side * pair_columns : (side + 1) * pair_columns]
-                nc.vector.tensor_tensor(windows[b][:].indirect(places), diff[:], sign[:], MULT)
+                nc.vector.tensor_tensor(windows[b][:].indirect(places), diff[:, block], sign[:, block], MULT)
             nc.sync.dma_start(out_blocks[b], windows[b][:])

@@ -38,12 +38,16 @@ def tile_symbranch_s_kernel(tc, base, hl, hr, offs, out):
         windows = [blocks.tile([P, nodes], F32, name="window") for b in range(n_blocks)]
 
         nc.sync.dma_start(offsets[:], offs)
+        base_due = []
         for first, behind in pieces:
             columns = slice(first * pairs, behind * pairs)
             nc.sync.dma_start(left[:, columns], hl_rows[:, columns])
             nc.sync.dma_start(right[:, columns], hr_rows[:, columns])
-            for b in range(first, behind):
+            for b in base_due:
                 nc.sync.dma_start(windows[b][:], base_blocks[b])
+            base_due = list(range(first, behind))
+        for b in base_due:
+            nc.sync.dma_start(windows[b][:], base_blocks[b])
 
         for first, behind in pieces:
             columns = slice(first * pairs, behind * pairs)
@@ -55,4 +59,4 @@ def tile_symbranch_s_kernel(tc, base, hl, hr, offs, out):
             for side in range(2):
                 places = offsets[:, side * pair_columns : (side + 1) * pair_columns]
                 nc.vector.tensor_tensor(windows[b][:].indirect(places), diff[:, block], sign[:, block], MULT)
-            nc.sync.dma_start(out_blocks[b], windows[b][:])
+            nc.scalar.dma_start(out_blocks[b], windows[b][:])

@@ -4,7 +4,7 @@ F32 = mybir.dt.float32
 U16 = mybir.dt.uint16
 MULT = mybir.AluOpType.mult
 P = 128
-PER_COLUMN = 16
+SIDES = 2
 
 
 def tile_symbranch_s_kernel(tc, base, hl, hr, offs, out):
@@ -12,7 +12,7 @@ def tile_symbranch_s_kernel(tc, base, hl, hr, offs, out):
     features, nodes = base.shape
     pairs = hl.shape[1]
     n_blocks = features // P
-    pair_columns = pairs // PER_COLUMN
+    placed = SIDES * pairs
 
     base_blocks = base.rearrange("(p b) s -> b p s", b=n_blocks)
     out_blocks = out.rearrange("(p b) s -> b p s", b=n_blocks)
@@ -34,7 +34,8 @@ def tile_symbranch_s_kernel(tc, base, hl, hr, offs, out):
         left = held.tile([P, n_blocks * pairs], F32, name="left")
         right = held.tile([P, n_blocks * pairs], F32, name="right")
         diff = held.tile([P, n_blocks * pairs], F32, name="diff")
-        sign = held.tile([P, n_blocks * pairs], F32, name="sign")
+        diff_placed = held.tile([P, n_blocks * placed], F32, name="diff_placed")
+        sign_placed = held.tile([P, n_blocks * placed], F32, name="sign_placed")
         windows = [blocks.tile([P, nodes], F32, name="window") for b in range(n_blocks)]
 
         nc.sync.dma_start(offsets[:], offs)
@@ -52,11 +53,23 @@ def tile_symbranch_s_kernel(tc, base, hl, hr, offs, out):
         for first, behind in pieces:
             columns = slice(first * pairs, behind * pairs)
             nc.vector.tensor_sub(diff[:, columns], left[:, columns], right[:, columns])
-            nc.scalar.sign(sign[:, columns], diff[:, columns])
+            read_for_each_side = (
+                diff[:, columns]
+                .rearrange("p (b m) -> p b m", m=pairs)
+                .unsqueeze(2)
+                .to_broadcast([P, behind - first, SIDES, pairs])
+            )
+            for function, laid_out in ((nc.scalar.sign, sign_placed), (nc.scalar.copy, diff_placed)):
+                function(
+                    laid_out[:, first * placed : behind * placed].rearrange(
+                        "p (b s m) -> p b s m", s=SIDES, m=pairs
+                    ),
+                    read_for_each_side,
+                )
 
         for b in range(n_blocks):
-            block = slice(b * pairs, (b + 1) * pairs)
-            for side in range(2):
-                places = offsets[:, side * pair_columns : (side + 1) * pair_columns]
-                nc.vector.tensor_tensor(windows[b][:].indirect(places), diff[:, block], sign[:, block], MULT)
+            values = slice(b * placed, (b + 1) * placed)
+            nc.vector.tensor_tensor(
+                windows[b][:].indirect(offsets[:]), diff_placed[:, values], sign_placed[:, values], MULT
+            )
             nc.scalar.dma_start(out_blocks[b], windows[b][:])

@@ -5,6 +5,8 @@ U16 = mybir.dt.uint16
 MULT = mybir.AluOpType.mult
 P = 128
 SIDES = 2
+LEFT = 0
+RIGHT = 1
 
 
 def tile_symbranch_s_kernel(tc, base, hl, hr, offs, out):
@@ -33,39 +35,34 @@ def tile_symbranch_s_kernel(tc, base, hl, hr, offs, out):
         offsets = held.tile([P, offs.shape[1]], U16, name="offsets")
         left = held.tile([P, n_blocks * pairs], F32, name="left")
         right = held.tile([P, n_blocks * pairs], F32, name="right")
-        diff = held.tile([P, n_blocks * pairs], F32, name="diff")
         diff_placed = held.tile([P, n_blocks * placed], F32, name="diff_placed")
         sign_placed = held.tile([P, n_blocks * placed], F32, name="sign_placed")
         windows = [blocks.tile([P, nodes], F32, name="window") for b in range(n_blocks)]
 
-        nc.sync.dma_start(offsets[:], offs)
-        base_due = []
+        for_scatters = [(offsets, offs)]
         for first, behind in pieces:
             columns = slice(first * pairs, behind * pairs)
             nc.sync.dma_start(left[:, columns], hl_rows[:, columns])
             nc.sync.dma_start(right[:, columns], hr_rows[:, columns])
-            for b in base_due:
-                nc.sync.dma_start(windows[b][:], base_blocks[b])
-            base_due = list(range(first, behind))
-        for b in base_due:
-            nc.sync.dma_start(windows[b][:], base_blocks[b])
+            for tile, source in for_scatters:
+                nc.sync.dma_start(tile[:], source)
+            for_scatters = [(windows[b], base_blocks[b]) for b in range(first, behind)]
+        for tile, source in for_scatters:
+            nc.sync.dma_start(tile[:], source)
 
         for first, behind in pieces:
             columns = slice(first * pairs, behind * pairs)
-            nc.vector.tensor_sub(diff[:, columns], left[:, columns], right[:, columns])
-            read_for_each_side = (
-                diff[:, columns]
-                .rearrange("p (b m) -> p b m", m=pairs)
-                .unsqueeze(2)
-                .to_broadcast([P, behind - first, SIDES, pairs])
+            values = slice(first * placed, behind * placed)
+            diffs = diff_placed[:, values].rearrange("p (b s m) -> p b s m", s=SIDES, m=pairs)
+            signs = sign_placed[:, values].rearrange("p (b s m) -> p b s m", s=SIDES, m=pairs)
+            nc.vector.tensor_sub(
+                diffs[:, :, LEFT, :],
+                left[:, columns].rearrange("p (b m) -> p b m", m=pairs),
+                right[:, columns].rearrange("p (b m) -> p b m", m=pairs),
             )
-            for function, laid_out in ((nc.scalar.sign, sign_placed), (nc.scalar.copy, diff_placed)):
-                function(
-                    laid_out[:, first * placed : behind * placed].rearrange(
-                        "p (b s m) -> p b s m", s=SIDES, m=pairs
-                    ),
-                    read_for_each_side,
-                )
+            nc.scalar.sign(signs, diffs[:, :, LEFT : LEFT + 1, :].to_broadcast([P, behind - first, SIDES, pairs]))
+            copy = nc.vector.tensor_copy if first == 0 else nc.scalar.copy
+            copy(diffs[:, :, RIGHT, :], diffs[:, :, LEFT, :])
 
         for b in range(n_blocks):
             values = slice(b * placed, (b + 1) * placed)

@@ -1,12 +1,15 @@
 import concourse.mybir as mybir
+from concourse.masks import make_identity
 
 F32 = mybir.dt.float32
 U16 = mybir.dt.uint16
 MULT = mybir.AluOpType.mult
+NOT_EQUAL = mybir.AluOpType.not_equal
 P = 128
 SIDES = 2
 LEFT = 0
 RIGHT = 1
+VECTOR_BLOCKS = 2
 
 
 def tile_symbranch_s_kernel(tc, base, hl, hr, offs, out):
@@ -21,16 +24,13 @@ def tile_symbranch_s_kernel(tc, base, hl, hr, offs, out):
     hl_rows = hl.rearrange("(p b) m -> p (b m)", b=n_blocks)
     hr_rows = hr.rearrange("(p b) m -> p (b m)", b=n_blocks)
 
-    pieces = []
-    first = 0
-    while first < n_blocks:
-        behind = first + max(first, 1)
-        pieces.append((first, behind))
-        first = behind
+    half = n_blocks // 2
+    pieces = [(b, b + 1) for b in range(half)] + [(b, b + 2) for b in range(half, n_blocks, 2)]
 
     with (
         tc.tile_pool(name="held", bufs=1) as held,
         tc.tile_pool(name="blocks", bufs=n_blocks) as blocks,
+        tc.psum_pool(name="sums", bufs=2) as sums,
     ):
         offsets = held.tile([P, offs.shape[1]], U16, name="offsets")
         left = held.tile([P, n_blocks * pairs], F32, name="left")
@@ -38,6 +38,14 @@ def tile_symbranch_s_kernel(tc, base, hl, hr, offs, out):
         diff_placed = held.tile([P, n_blocks * placed], F32, name="diff_placed")
         sign_placed = held.tile([P, n_blocks * placed], F32, name="sign_placed")
         windows = [blocks.tile([P, nodes], F32, name="window") for b in range(n_blocks)]
+
+        plus = held.tile([P, P], F32, name="plus")
+        minus = held.tile([P, P], F32, name="minus")
+        make_identity(nc, plus[:])
+        nc.gpsimd.memset(minus[:], 0.0)
+        nc.gpsimd.affine_select(
+            out=minus[:], in_=minus[:], compare_op=NOT_EQUAL, fill=-1.0, base=0, pattern=[[-1, P]], channel_multiplier=1
+        )
 
         for_scatters = [(offsets, offs)]
         for first, behind in pieces:
@@ -53,20 +61,29 @@ def tile_symbranch_s_kernel(tc, base, hl, hr, offs, out):
         for first, behind in pieces:
             columns = slice(first * pairs, behind * pairs)
             values = slice(first * placed, behind * placed)
+            both_sides = [P, behind - first, SIDES, pairs]
             diffs = diff_placed[:, values].rearrange("p (b s m) -> p b s m", s=SIDES, m=pairs)
             signs = sign_placed[:, values].rearrange("p (b s m) -> p b s m", s=SIDES, m=pairs)
-            nc.vector.tensor_sub(
-                diffs[:, :, LEFT, :],
-                left[:, columns].rearrange("p (b m) -> p b m", m=pairs),
-                right[:, columns].rearrange("p (b m) -> p b m", m=pairs),
-            )
-            nc.scalar.sign(signs, diffs[:, :, LEFT : LEFT + 1, :].to_broadcast([P, behind - first, SIDES, pairs]))
-            copy = nc.vector.tensor_copy if first == 0 else nc.scalar.copy
-            copy(diffs[:, :, RIGHT, :], diffs[:, :, LEFT, :])
+            if first < VECTOR_BLOCKS:
+                nc.vector.tensor_sub(
+                    diffs[:, :, LEFT, :],
+                    left[:, columns].rearrange("p (b m) -> p b m", m=pairs),
+                    right[:, columns].rearrange("p (b m) -> p b m", m=pairs),
+                )
+                nc.scalar.sign(signs, diffs[:, :, LEFT : LEFT + 1, :].to_broadcast(both_sides))
+                copy = nc.vector.tensor_copy if first == 0 else nc.scalar.copy
+                copy(diffs[:, :, RIGHT, :], diffs[:, :, LEFT, :])
+            else:
+                diff_sum = sums.tile([P, (behind - first) * pairs], F32, name="diff_sum")
+                nc.tensor.matmul(diff_sum[:], plus[:], left[:, columns], start=True, stop=False)
+                nc.tensor.matmul(diff_sum[:], minus[:], right[:, columns], start=False, stop=True)
+                twice = diff_sum[:].rearrange("p (b m) -> p b m", m=pairs).unsqueeze(2).to_broadcast(both_sides)
+                nc.scalar.sign(signs, twice)
+                nc.scalar.copy(diffs, twice)
 
         for b in range(n_blocks):
             values = slice(b * placed, (b + 1) * placed)
             nc.vector.tensor_tensor(
                 windows[b][:].indirect(offsets[:]), diff_placed[:, values], sign_placed[:, values], MULT
             )
-            nc.scalar.dma_start(out_blocks[b], windows[b][:])
+            nc.sync.dma_start(out_blocks[b], windows[b][:])

@@ -25,12 +25,13 @@ def tile_symbranch_s_kernel(tc, base, hl, hr, offs, out):
     hr_rows = hr.rearrange("(p b) m -> p (b m)", b=n_blocks)
 
     half = n_blocks // 2
-    pieces = [(b, b + 1) for b in range(half)] + [(b, b + 2) for b in range(half, n_blocks, 2)]
+    loaded_pieces = [(b, b + 1) for b in range(half)] + [(b, b + 2) for b in range(half, n_blocks, 2)]
+    pieces = [(b, b + 1) for b in range(n_blocks)]
 
     with (
         tc.tile_pool(name="held", bufs=1) as held,
         tc.tile_pool(name="blocks", bufs=n_blocks) as blocks,
-        tc.psum_pool(name="sums", bufs=2) as sums,
+        tc.psum_pool(name="sums", bufs=4) as sums,
     ):
         offsets = held.tile([P, offs.shape[1]], U16, name="offsets")
         left = held.tile([P, n_blocks * pairs], F32, name="left")
@@ -48,7 +49,7 @@ def tile_symbranch_s_kernel(tc, base, hl, hr, offs, out):
         )
 
         for_scatters = [(offsets, offs)]
-        for first, behind in pieces:
+        for first, behind in loaded_pieces:
             columns = slice(first * pairs, behind * pairs)
             nc.sync.dma_start(left[:, columns], hl_rows[:, columns])
             nc.sync.dma_start(right[:, columns], hr_rows[:, columns])

@@ -24,8 +24,7 @@ def tile_symbranch_s_kernel(tc, base, hl, hr, offs, out):
     hl_rows = hl.rearrange("(p b) m -> p (b m)", b=n_blocks)
     hr_rows = hr.rearrange("(p b) m -> p (b m)", b=n_blocks)
 
-    half = n_blocks // 2
-    loaded_pieces = [(b, b + 1) for b in range(half)] + [(b, b + 2) for b in range(half, n_blocks, 2)]
+    loaded_pieces = [(b, b + 1) for b in range(n_blocks - 2)] + [(n_blocks - 2, n_blocks)]
     pieces = [(b, b + 1) for b in range(n_blocks)]
 
     with (

@@ -86,4 +86,5 @@ def tile_symbranch_s_kernel(tc, base, hl, hr, offs, out):
             nc.vector.tensor_tensor(
                 windows[b][:].indirect(offsets[:]), diff_placed[:, values], sign_placed[:, values], MULT
             )
-            nc.sync.dma_start(out_blocks[b], windows[b][:])
+            store_queue = nc.scalar if b == n_blocks - 3 else nc.sync
+            store_queue.dma_start(out_blocks[b], windows[b][:])

@@ -3,13 +3,15 @@ from concourse.masks import make_identity
 
 F32 = mybir.dt.float32
 U16 = mybir.dt.uint16
+I32 = mybir.dt.int32
 MULT = mybir.AluOpType.mult
 NOT_EQUAL = mybir.AluOpType.not_equal
+AND = mybir.AluOpType.bitwise_and
+OR = mybir.AluOpType.bitwise_or
+SIGN_BIT = -(2**31)
+ONE_BITS = 0x3F800000
 P = 128
 SIDES = 2
-LEFT = 0
-RIGHT = 1
-VECTOR_BLOCKS = 2
 
 
 def tile_symbranch_s_kernel(tc, base, hl, hr, offs, out):
@@ -64,15 +66,15 @@ def tile_symbranch_s_kernel(tc, base, hl, hr, offs, out):
             both_sides = [P, behind - first, SIDES, pairs]
             diffs = diff_placed[:, values].rearrange("p (b s m) -> p b s m", s=SIDES, m=pairs)
             signs = sign_placed[:, values].rearrange("p (b s m) -> p b s m", s=SIDES, m=pairs)
-            if first < VECTOR_BLOCKS:
+            if first == 0:
                 nc.vector.tensor_sub(
-                    diffs[:, :, LEFT, :],
-                    left[:, columns].rearrange("p (b m) -> p b m", m=pairs),
-                    right[:, columns].rearrange("p (b m) -> p b m", m=pairs),
+                    diffs,
+                    left[:, columns].rearrange("p (b m) -> p b m", m=pairs).unsqueeze(2).to_broadcast(both_sides),
+                    right[:, columns].rearrange("p (b m) -> p b m", m=pairs).unsqueeze(2).to_broadcast(both_sides),
                 )
-                nc.scalar.sign(signs, diffs[:, :, LEFT : LEFT + 1, :].to_broadcast(both_sides))
-                copy = nc.vector.tensor_copy if first == 0 else nc.scalar.copy
-                copy(diffs[:, :, RIGHT, :], diffs[:, :, LEFT, :])
+                nc.vector.tensor_scalar(
+                    sign_placed[:, values].bitcast(I32), diff_placed[:, values].bitcast(I32), SIGN_BIT, ONE_BITS, AND, OR
+                )
             else:
                 diff_sum = sums.tile([P, (behind - first) * pairs], F32, name="diff_sum")
                 nc.tensor.matmul(diff_sum[:], plus[:], left[:, columns], start=True, stop=False)

@@ -49,16 +49,16 @@ def tile_symbranch_s_kernel(tc, base, hl, hr, offs, out):
             out=minus[:], in_=minus[:], compare_op=NOT_EQUAL, fill=-1.0, base=0, pattern=[[-1, P]], channel_multiplier=1
         )
 
-        for_scatters = [(offsets, offs)]
         for first, behind in loaded_pieces:
             columns = slice(first * pairs, behind * pairs)
             nc.sync.dma_start(left[:, columns], hl_rows[:, columns])
             nc.sync.dma_start(right[:, columns], hr_rows[:, columns])
-            for tile, source in for_scatters:
-                nc.sync.dma_start(tile[:], source)
-            for_scatters = [(windows[b], base_blocks[b]) for b in range(first, behind)]
-        for tile, source in for_scatters:
-            nc.sync.dma_start(tile[:], source)
+            if first > 0:
+                nc.sync.dma_start(windows[first - 1][:], base_blocks[first - 1])
+            if first == 1:
+                nc.sync.dma_start(offsets[:], offs)
+        for b in range(n_blocks - 2, n_blocks):
+            nc.sync.dma_start(windows[b][:], base_blocks[b])
 
         for first, behind in pieces:
             columns = slice(first * pairs, behind * pairs)

@@ -51,8 +51,9 @@ def tile_symbranch_s_kernel(tc, base, hl, hr, offs, out):
 
         for first, behind in loaded_pieces:
             columns = slice(first * pairs, behind * pairs)
+            hr_queue = nc.scalar if first <= 1 else nc.sync
             nc.sync.dma_start(left[:, columns], hl_rows[:, columns])
-            nc.sync.dma_start(right[:, columns], hr_rows[:, columns])
+            hr_queue.dma_start(right[:, columns], hr_rows[:, columns])
             if first > 0:
                 nc.sync.dma_start(windows[first - 1][:], base_blocks[first - 1])
             if first == 1:

@@ -11,6 +11,7 @@ OR = mybir.AluOpType.bitwise_or
 SIGN_BIT = -(2**31)
 ONE_BITS = 0x3F800000
 P = 128
+SCALAR_LOADS = 2
 SIDES = 2
 
 
@@ -26,7 +27,6 @@ def tile_symbranch_s_kernel(tc, base, hl, hr, offs, out):
     hl_rows = hl.rearrange("(p b) m -> p (b m)", b=n_blocks)
     hr_rows = hr.rearrange("(p b) m -> p (b m)", b=n_blocks)
 
-    loaded_pieces = [(b, b + 1) for b in range(n_blocks - 2)] + [(n_blocks - 2, n_blocks)]
     pieces = [(b, b + 1) for b in range(n_blocks)]
 
     with (
@@ -49,17 +49,18 @@ def tile_symbranch_s_kernel(tc, base, hl, hr, offs, out):
             out=minus[:], in_=minus[:], compare_op=NOT_EQUAL, fill=-1.0, base=0, pattern=[[-1, P]], channel_multiplier=1
         )
 
-        for first, behind in loaded_pieces:
-            columns = slice(first * pairs, behind * pairs)
-            hr_queue = nc.scalar if first <= 1 else nc.sync
-            nc.sync.dma_start(left[:, columns], hl_rows[:, columns])
-            hr_queue.dma_start(right[:, columns], hr_rows[:, columns])
-            if first > 0:
-                nc.sync.dma_start(windows[first - 1][:], base_blocks[first - 1])
-            if first == 1:
+        for b in range(n_blocks):
+            if b < n_blocks - 1:
+                hl_columns = slice(b * pairs, (n_blocks if b == n_blocks - 2 else b + 1) * pairs)
+                nc.sync.dma_start(left[:, hl_columns], hl_rows[:, hl_columns])
+            hr_columns = slice(b * pairs, (b + 1) * pairs)
+            hr_queue = nc.scalar if b < SCALAR_LOADS else nc.sync
+            hr_queue.dma_start(right[:, hr_columns], hr_rows[:, hr_columns])
+            if b > 0:
+                nc.sync.dma_start(windows[b - 1][:], base_blocks[b - 1])
+            if b == 1:
                 nc.sync.dma_start(offsets[:], offs)
-        for b in range(n_blocks - 2, n_blocks):
-            nc.sync.dma_start(windows[b][:], base_blocks[b])
+        nc.sync.dma_start(windows[n_blocks - 1][:], base_blocks[n_blocks - 1])
 
         for first, behind in pieces:
             columns = slice(first * pairs, behind * pairs)
@@ -89,5 +90,4 @@ def tile_symbranch_s_kernel(tc, base, hl, hr, offs, out):
             nc.vector.tensor_tensor(
                 windows[b][:].indirect(offsets[:]), diff_placed[:, values], sign_placed[:, values], MULT
             )
-            store_queue = nc.scalar if b == n_blocks - 3 else nc.sync
-            store_queue.dma_start(out_blocks[b], windows[b][:])
+            nc.sync.dma_start(out_blocks[b], windows[b][:])

@@ -1,5 +1,4 @@
 import concourse.mybir as mybir
-from concourse.masks import make_identity
 
 F32 = mybir.dt.float32
 U16 = mybir.dt.uint16
@@ -43,11 +42,17 @@ def tile_symbranch_s_kernel(tc, base, hl, hr, offs, out):
 
         plus = held.tile([P, P], F32, name="plus")
         minus = held.tile([P, P], F32, name="minus")
-        make_identity(nc, plus[:])
-        nc.gpsimd.memset(minus[:], 0.0)
-        nc.gpsimd.affine_select(
-            out=minus[:], in_=minus[:], compare_op=NOT_EQUAL, fill=-1.0, base=0, pattern=[[-1, P]], channel_multiplier=1
-        )
+        for matrix, diagonal in ((plus, 1.0), (minus, -1.0)):
+            nc.vector.memset(matrix[:], 0.0)
+            nc.gpsimd.affine_select(
+                out=matrix[:],
+                in_=matrix[:],
+                compare_op=NOT_EQUAL,
+                fill=diagonal,
+                base=0,
+                pattern=[[-1, P]],
+                channel_multiplier=1,
+            )
 
         for b in range(n_blocks):
             if b < n_blocks - 1:

@@ -12,6 +12,8 @@ ONE_BITS = 0x3F800000
 P = 128
 SCALAR_LOADS = 2
 SIDES = 2
+LEFT = 0
+RIGHT = 1
 
 
 def tile_symbranch_s_kernel(tc, base, hl, hr, offs, out):
@@ -26,7 +28,6 @@ def tile_symbranch_s_kernel(tc, base, hl, hr, offs, out):
     hl_rows = hl.rearrange("(p b) m -> p (b m)", b=n_blocks)
     hr_rows = hr.rearrange("(p b) m -> p (b m)", b=n_blocks)
 
-    pieces = [(b, b + 1) for b in range(n_blocks)]
 
     with (
         tc.tile_pool(name="held", bufs=1) as held,
@@ -67,26 +68,30 @@ def tile_symbranch_s_kernel(tc, base, hl, hr, offs, out):
                 nc.sync.dma_start(offsets[:], offs)
         nc.sync.dma_start(windows[n_blocks - 1][:], base_blocks[n_blocks - 1])
 
-        for first, behind in pieces:
-            columns = slice(first * pairs, behind * pairs)
-            values = slice(first * placed, behind * placed)
-            both_sides = [P, behind - first, SIDES, pairs]
-            diffs = diff_placed[:, values].rearrange("p (b s m) -> p b s m", s=SIDES, m=pairs)
-            signs = sign_placed[:, values].rearrange("p (b s m) -> p b s m", s=SIDES, m=pairs)
-            if first == 0:
+        for b in range(n_blocks):
+            columns = slice(b * pairs, (b + 1) * pairs)
+            values = slice(b * placed, (b + 1) * placed)
+            both_sides = [P, SIDES, pairs]
+            diffs = diff_placed[:, values].rearrange("p (s m) -> p s m", s=SIDES)
+            signs = sign_placed[:, values].rearrange("p (s m) -> p s m", s=SIDES)
+            if b == 0:
                 nc.vector.tensor_sub(
                     diffs,
-                    left[:, columns].rearrange("p (b m) -> p b m", m=pairs).unsqueeze(2).to_broadcast(both_sides),
-                    right[:, columns].rearrange("p (b m) -> p b m", m=pairs).unsqueeze(2).to_broadcast(both_sides),
+                    left[:, columns].unsqueeze(1).to_broadcast(both_sides),
+                    right[:, columns].unsqueeze(1).to_broadcast(both_sides),
                 )
+            elif b == 1:
+                nc.vector.tensor_sub(diffs[:, LEFT], left[:, columns], right[:, columns])
+                nc.scalar.sign(signs, diffs[:, LEFT : LEFT + 1].to_broadcast(both_sides))
+                nc.scalar.copy(diffs[:, RIGHT], diffs[:, LEFT])
                 nc.vector.tensor_scalar(
-                    sign_placed[:, values].bitcast(I32), diff_placed[:, values].bitcast(I32), SIGN_BIT, ONE_BITS, AND, OR
+                    sign_placed[:, :placed].bitcast(I32), diff_placed[:, :placed].bitcast(I32), SIGN_BIT, ONE_BITS, AND, OR
                 )
             else:
-                diff_sum = sums.tile([P, (behind - first) * pairs], F32, name="diff_sum")
+                diff_sum = sums.tile([P, pairs], F32, name="diff_sum")
                 nc.tensor.matmul(diff_sum[:], plus[:], left[:, columns], start=True, stop=False)
                 nc.tensor.matmul(diff_sum[:], minus[:], right[:, columns], start=False, stop=True)
-                twice = diff_sum[:].rearrange("p (b m) -> p b m", m=pairs).unsqueeze(2).to_broadcast(both_sides)
+                twice = diff_sum[:].unsqueeze(1).to_broadcast(both_sides)
                 nc.scalar.sign(signs, twice)
                 nc.scalar.copy(diffs, twice)
 

@@ -10,7 +10,7 @@ OR = mybir.AluOpType.bitwise_or
 SIGN_BIT = -(2**31)
 ONE_BITS = 0x3F800000
 P = 128
-SCALAR_LOADS = 2
+VECTOR_BLOCKS = 2
 SIDES = 2
 LEFT = 0
 RIGHT = 1
@@ -55,18 +55,22 @@ def tile_symbranch_s_kernel(tc, base, hl, hr, offs, out):
                 channel_multiplier=1,
             )
 
-        for b in range(n_blocks):
-            if b < n_blocks - 1:
-                hl_columns = slice(b * pairs, (n_blocks if b == n_blocks - 2 else b + 1) * pairs)
-                nc.sync.dma_start(left[:, hl_columns], hl_rows[:, hl_columns])
-            hr_columns = slice(b * pairs, (b + 1) * pairs)
-            hr_queue = nc.scalar if b < SCALAR_LOADS else nc.sync
-            hr_queue.dma_start(right[:, hr_columns], hr_rows[:, hr_columns])
-            if b > 0:
-                nc.sync.dma_start(windows[b - 1][:], base_blocks[b - 1])
-            if b == 1:
-                nc.sync.dma_start(offsets[:], offs)
-        nc.sync.dma_start(windows[n_blocks - 1][:], base_blocks[n_blocks - 1])
+        for b in range(VECTOR_BLOCKS):
+            columns = slice(b * pairs, (b + 1) * pairs)
+            nc.sync.dma_start(left[:, columns], hl_rows[:, columns])
+            nc.scalar.dma_start(right[:, columns], hr_rows[:, columns])
+        nc.sync.dma_start(windows[0][:], base_blocks[0])
+        nc.sync.dma_start(offsets[:], offs)
+        for b in range(1, n_blocks):
+            nc.sync.dma_start(windows[b][:], base_blocks[b])
+            ahead = b + 1
+            if ahead < n_blocks - 1:
+                behind = n_blocks if ahead == n_blocks - 2 else ahead + 1
+                columns = slice(ahead * pairs, behind * pairs)
+                nc.sync.dma_start(left[:, columns], hl_rows[:, columns])
+            if ahead < n_blocks:
+                columns = slice(ahead * pairs, (ahead + 1) * pairs)
+                nc.sync.dma_start(right[:, columns], hr_rows[:, columns])
 
         for b in range(n_blocks):
             columns = slice(b * pairs, (b + 1) * pairs)

import concourse.mybir as mybir

F32 = mybir.dt.float32
U16 = mybir.dt.uint16
I32 = mybir.dt.int32
MULT = mybir.AluOpType.mult
NOT_EQUAL = mybir.AluOpType.not_equal
AND = mybir.AluOpType.bitwise_and
OR = mybir.AluOpType.bitwise_or
SIGN_BIT = -(2**31)
ONE_BITS = 0x3F800000
P = 128
VECTOR_BLOCKS = 2
SIDES = 2
LEFT = 0
RIGHT = 1


def tile_symbranch_s_kernel(tc, base, hl, hr, offs, out):
    nc = tc.nc
    features, nodes = base.shape
    pairs = hl.shape[1]
    n_blocks = features // P
    placed = SIDES * pairs

    base_blocks = base.rearrange("(p b) s -> b p s", b=n_blocks)
    out_blocks = out.rearrange("(p b) s -> b p s", b=n_blocks)
    hl_rows = hl.rearrange("(p b) m -> p (b m)", b=n_blocks)
    hr_rows = hr.rearrange("(p b) m -> p (b m)", b=n_blocks)


    with (
        tc.tile_pool(name="held", bufs=1) as held,
        tc.tile_pool(name="blocks", bufs=n_blocks) as blocks,
        tc.psum_pool(name="sums", bufs=4) as sums,
    ):
        offsets = held.tile([P, offs.shape[1]], U16, name="offsets")
        left = held.tile([P, n_blocks * pairs], F32, name="left")
        right = held.tile([P, n_blocks * pairs], F32, name="right")
        diff_placed = held.tile([P, n_blocks * placed], F32, name="diff_placed")
        sign_placed = held.tile([P, n_blocks * placed], F32, name="sign_placed")
        windows = [blocks.tile([P, nodes], F32, name="window") for b in range(n_blocks)]

        plus = held.tile([P, P], F32, name="plus")
        minus = held.tile([P, P], F32, name="minus")
        for matrix, diagonal in ((plus, 1.0), (minus, -1.0)):
            nc.vector.memset(matrix[:], 0.0)
            nc.gpsimd.affine_select(
                out=matrix[:],
                in_=matrix[:],
                compare_op=NOT_EQUAL,
                fill=diagonal,
                base=0,
                pattern=[[-1, P]],
                channel_multiplier=1,
            )

        for b in range(VECTOR_BLOCKS):
            columns = slice(b * pairs, (b + 1) * pairs)
            nc.sync.dma_start(left[:, columns], hl_rows[:, columns])
            nc.scalar.dma_start(right[:, columns], hr_rows[:, columns])
        nc.sync.dma_start(windows[0][:], base_blocks[0])
        nc.sync.dma_start(offsets[:], offs)
        for b in range(1, n_blocks):
            nc.sync.dma_start(windows[b][:], base_blocks[b])
            ahead = b + 1
            if ahead < n_blocks - 1:
                behind = n_blocks if ahead == n_blocks - 2 else ahead + 1
                columns = slice(ahead * pairs, behind * pairs)
                nc.sync.dma_start(left[:, columns], hl_rows[:, columns])
            if ahead < n_blocks:
                columns = slice(ahead * pairs, (ahead + 1) * pairs)
                nc.sync.dma_start(right[:, columns], hr_rows[:, columns])

        for b in range(n_blocks):
            columns = slice(b * pairs, (b + 1) * pairs)
            values = slice(b * placed, (b + 1) * placed)
            both_sides = [P, SIDES, pairs]
            diffs = diff_placed[:, values].rearrange("p (s m) -> p s m", s=SIDES)
            signs = sign_placed[:, values].rearrange("p (s m) -> p s m", s=SIDES)
            if b == 0:
                nc.vector.tensor_sub(
                    diffs,
                    left[:, columns].unsqueeze(1).to_broadcast(both_sides),
                    right[:, columns].unsqueeze(1).to_broadcast(both_sides),
                )
            elif b == 1:
                nc.vector.tensor_sub(diffs[:, LEFT], left[:, columns], right[:, columns])
                nc.scalar.sign(signs, diffs[:, LEFT : LEFT + 1].to_broadcast(both_sides))
                nc.scalar.copy(diffs[:, RIGHT], diffs[:, LEFT])
                nc.vector.tensor_scalar(
                    sign_placed[:, :placed].bitcast(I32), diff_placed[:, :placed].bitcast(I32), SIGN_BIT, ONE_BITS, AND, OR
                )
            else:
                diff_sum = sums.tile([P, pairs], F32, name="diff_sum")
                nc.tensor.matmul(diff_sum[:], plus[:], left[:, columns], start=True, stop=False)
                nc.tensor.matmul(diff_sum[:], minus[:], right[:, columns], start=False, stop=True)
                twice = diff_sum[:].unsqueeze(1).to_broadcast(both_sides)
                nc.scalar.sign(signs, twice)
                nc.scalar.copy(diffs, twice)

        for b in range(n_blocks):
            values = slice(b * placed, (b + 1) * placed)
            nc.vector.tensor_tensor(
                windows[b][:].indirect(offsets[:]), diff_placed[:, values], sign_placed[:, values], MULT
            )
            nc.sync.dma_start(out_blocks[b], windows[b][:])
